import numpy as np
import ml_dtypes

BF16 = ml_dtypes.bfloat16


def bf(x):
    return np.asarray(x, np.float32).astype(BF16)


def f32(x):
    return np.asarray(x, np.float32)


def f64(x):
    return np.asarray(x).astype(np.float64)


def striped(idx):
    return np.tile(idx.reshape(-1, 16).T, (8, 1))


C, S, N, M, H, K = 768, 256, 1024, 256, 128, 8
EPS = 1e-5


def setup_inputs():
    idx = np.concatenate([np.random.permutation(S)[:H] for _ in range(K)])
    return {"tok_emb": f32(np.random.standard_normal((C, S))), "pos_emb": f32(np.random.standard_normal((C, N))), "rmsf_w": f32(1.0 + 0.1 * np.random.standard_normal((C, 1))), "head_w": bf(np.random.standard_normal((C, M)) / np.sqrt(C)), "offs": striped(idx)}


def reference(tok_emb, pos_emb, rmsf_w, head_w, offs):
    idx = offs[:16].T.reshape(-1)
    x = f64(tok_emb)[:, idx] + f64(pos_emb)
    r = 1.0 / np.sqrt(np.mean(x * x, axis=0, keepdims=True) + EPS)
    h = x * r * f64(rmsf_w)
    return f64(head_w).T @ h

@@ -1,0 +1,82 @@
+import concourse.mybir as mybir
+
+F32, BF16, U16 = mybir.dt.float32, mybir.dt.bfloat16, mybir.dt.uint16
+ADD, MULT = mybir.AluOpType.add, mybir.AluOpType.mult
+ACT = mybir.ActivationFunctionType
+
+P = 128
+C, S, N, M = 768, 256, 1024, 256
+EPS = 1e-5
+CB = C // P
+VB = M // P
+PIECE = S
+NP = N // PIECE
+FLOPS = 2 * C * M * N
+
+
+def tile_metajanusrrpram_kernel(tc, tok_emb, pos_emb, rmsf_w, head_w, offs, out):
+    nc = tc.nc
+    with (
+        tc.tile_pool(name="held", bufs=1) as held,
+        tc.tile_pool(name="pieces", bufs=NP) as pieces,
+        tc.psum_pool(name="psum", bufs=2) as psum,
+    ):
+        offsets = held.tile([P, N // 16], U16, name="offsets")
+        nc.sync.dma_start(offsets[:], offs)
+
+        tables = [held.tile([P, S], F32, name=f"table{b}") for b in range(CB)]
+        pos = [held.tile([P, CB, PIECE], F32, name=f"pos{k}") for k in range(NP)]
+        for b in range(CB):
+            nc.sync.dma_start(tables[b][:], tok_emb[b * P : (b + 1) * P, :])
+            nc.sync.dma_start(pos[0][:, b, :], pos_emb[b * P : (b + 1) * P, 0:PIECE])
+        gain = held.tile([P, CB], F32, name="gain")
+        with nc.allow_non_contiguous_dma(reason="768 gains, one to a partition and block"):
+            nc.sync.dma_start(gain[:], rmsf_w.rearrange("(b p) o -> p (b o)", p=P))
+        head = held.tile([P, CB, M], BF16, name="head")
+        nc.sync.dma_start(head[:], head_w.rearrange("(b p) v -> p b v", p=P))
+        for k in range(1, NP):
+            for b in range(CB):
+                nc.sync.dma_start(
+                    pos[k][:, b, :], pos_emb[b * P : (b + 1) * P, k * PIECE : (k + 1) * PIECE]
+                )
+
+        ones = held.tile([P, P], BF16, name="ones")
+        nc.vector.memset(ones[:], 1.0)
+        eps = held.tile([P, 1], F32, name="eps")
+        nc.vector.memset(eps[:], EPS)
+
+        def embed(k):
+            x = pieces.tile([P, CB, PIECE], F32, name="x")
+            squares = pieces.tile([P, CB, PIECE], BF16, name="squares")
+            sumsq = psum.tile([P, PIECE], F32, name="sumsq")
+            piece_offsets = offsets[:, k * (PIECE // 16) : (k + 1) * (PIECE // 16)]
+            for b in range(CB):
+                nc.vector.tensor_tensor(
+                    x[:, b, :], tables[b][:].indirect(piece_offsets), pos[k][:, b, :], ADD
+                )
+                nc.scalar.activation(squares[:, b, :], x[:, b, :], ACT.Square)
+                nc.tensor.matmul(sumsq[:], ones[:], squares[:, b, :], start=(b == 0), stop=(b == CB - 1))
+            return x, sumsq
+
+        def project(k, x, sumsq):
+            r = pieces.tile([P, PIECE], F32, name="r")
+            nc.scalar.activation(r[:], sumsq[:], ACT.Abs_reciprocal_sqrt, bias=eps[:], scale=1.0 / C)
+            h = pieces.tile([P, CB, PIECE], BF16, name="h")
+            for b in range(CB):
+                nc.vector.scalar_tensor_tensor(h[:, b, :], x[:, b, :], gain[:, b : b + 1], r[:], MULT, MULT)
+            for v in range(VB):
+                logits = psum.tile([P, PIECE], F32, name=f"logits{v}")
+                for b in range(CB):
+                    nc.tensor.matmul(
+                        logits[:], head[:, b, v * P : (v + 1) * P], h[:, b, :],
+                        start=(b == 0), stop=(b == CB - 1),
+                    )
+                staged = pieces.tile([P, PIECE], F32, name=f"staged{v}")
+                nc.scalar.copy(staged[:], logits[:])
+                nc.sync.dma_start(out[v * P : (v + 1) * P, k * PIECE : (k + 1) * PIECE], staged[:])
+
+        embedded = embed(0)
+        for k in range(NP):
+            following = embed(k + 1) if k + 1 < NP else None
+            project(k, *embedded)
+            embedded = following

@@ -48,35 +48,34 @@ def tile_metajanusrrpram_kernel(tc, tok_emb, pos_emb, rmsf_w, head_w, offs, out)
         def embed(k):
             x = pieces.tile([P, CB, PIECE], F32, name="x")
             squares = pieces.tile([P, CB, PIECE], BF16, name="squares")
+            gained = pieces.tile([P, CB, PIECE], BF16, name="gained")
             sumsq = psum.tile([P, PIECE], F32, name="sumsq")
+            logits = [psum.tile([P, PIECE], F32, name=f"logits{v}") for v in range(VB)]
             piece_offsets = offsets[:, k * (PIECE // 16) : (k + 1) * (PIECE // 16)]
             for b in range(CB):
+                first, last = b == 0, b == CB - 1
                 nc.vector.tensor_tensor(
                     x[:, b, :], tables[b][:].indirect(piece_offsets), pos[k][:, b, :], ADD
                 )
                 nc.scalar.activation(squares[:, b, :], x[:, b, :], ACT.Square)
-                nc.tensor.matmul(sumsq[:], ones[:], squares[:, b, :], start=(b == 0), stop=(b == CB - 1))
-            return x, sumsq
+                nc.scalar.activation(gained[:, b, :], x[:, b, :], ACT.Copy, scale=gain[:, b : b + 1])
+                nc.tensor.matmul(sumsq[:], ones[:], squares[:, b, :], start=first, stop=last)
+                for v in range(VB):
+                    nc.tensor.matmul(
+                        logits[v][:], head[:, b, v * P : (v + 1) * P], gained[:, b, :], start=first, stop=last
+                    )
+            return sumsq, logits
 
-        def project(k, x, sumsq):
+        def normalise(k, sumsq, logits):
             r = pieces.tile([P, PIECE], F32, name="r")
             nc.scalar.activation(r[:], sumsq[:], ACT.Abs_reciprocal_sqrt, bias=eps[:], scale=1.0 / C)
-            h = pieces.tile([P, CB, PIECE], BF16, name="h")
-            for b in range(CB):
-                nc.vector.scalar_tensor_tensor(h[:, b, :], x[:, b, :], gain[:, b : b + 1], r[:], MULT, MULT)
             for v in range(VB):
-                logits = psum.tile([P, PIECE], F32, name=f"logits{v}")
-                for b in range(CB):
-                    nc.tensor.matmul(
-                        logits[:], head[:, b, v * P : (v + 1) * P], h[:, b, :],
-                        start=(b == 0), stop=(b == CB - 1),
-                    )
                 staged = pieces.tile([P, PIECE], F32, name=f"staged{v}")
-                nc.scalar.copy(staged[:], logits[:])
+                nc.vector.tensor_tensor(staged[:], logits[v][:], r[:], MULT)
                 nc.sync.dma_start(out[v * P : (v + 1) * P, k * PIECE : (k + 1) * PIECE], staged[:])
 
         embedded = embed(0)
         for k in range(NP):
             following = embed(k + 1) if k + 1 < NP else None
-            project(k, *embedded)
+            normalise(k, *embedded)
             embedded = following

@@ -64,11 +64,11 @@ def tile_metajanusrrpram_kernel(tc, tok_emb, pos_emb, rmsf_w, head_w, offs, out)
                     nc.tensor.matmul(
                         logits[v][:], head[:, b, v * P : (v + 1) * P], gained[:, b, :], start=first, stop=last
                     )
-            return sumsq, logits
-
-        def normalise(k, sumsq, logits):
             r = pieces.tile([P, PIECE], F32, name="r")
             nc.scalar.activation(r[:], sumsq[:], ACT.Abs_reciprocal_sqrt, bias=eps[:], scale=1.0 / C)
+            return r, logits
+
+        def normalise(k, r, logits):
             for v in range(VB):
                 staged = pieces.tile([P, PIECE], F32, name=f"staged{v}")
                 nc.vector.tensor_tensor(staged[:], logits[v][:], r[:], MULT)

@@ -23,22 +23,22 @@ def tile_metajanusrrpram_kernel(tc, tok_emb, pos_emb, rmsf_w, head_w, offs, out)
     ):
         offsets = held.tile([P, N // 16], U16, name="offsets")
         nc.sync.dma_start(offsets[:], offs)
-
-        tables = [held.tile([P, S], F32, name=f"table{b}") for b in range(CB)]
-        pos = [held.tile([P, CB, PIECE], F32, name=f"pos{k}") for k in range(NP)]
-        for b in range(CB):
-            nc.sync.dma_start(tables[b][:], tok_emb[b * P : (b + 1) * P, :])
-            nc.sync.dma_start(pos[0][:, b, :], pos_emb[b * P : (b + 1) * P, 0:PIECE])
         gain = held.tile([P, CB], F32, name="gain")
         with nc.allow_non_contiguous_dma(reason="768 gains, one to a partition and block"):
             nc.sync.dma_start(gain[:], rmsf_w.rearrange("(b p) o -> p (b o)", p=P))
+
+        tables = [held.tile([P, S], F32, name=f"table{b}") for b in range(CB)]
+        pos = [held.tile([P, CB, PIECE], F32, name=f"pos{k}") for k in range(NP)]
         head = held.tile([P, CB, M], BF16, name="head")
-        nc.sync.dma_start(head[:], head_w.rearrange("(b p) v -> p b v", p=P))
-        for k in range(1, NP):
+        for k in range(NP):
             for b in range(CB):
+                if k == 0:
+                    nc.sync.dma_start(tables[b][:], tok_emb[b * P : (b + 1) * P, :])
                 nc.sync.dma_start(
                     pos[k][:, b, :], pos_emb[b * P : (b + 1) * P, k * PIECE : (k + 1) * PIECE]
                 )
+            if k == 1:
+                nc.sync.dma_start(head[:], head_w.rearrange("(b p) v -> p b v", p=P))
 
         ones = held.tile([P, P], BF16, name="ones")
         nc.vector.memset(ones[:], 1.0)

@@ -44,6 +44,8 @@ def tile_metajanusrrpram_kernel(tc, tok_emb, pos_emb, rmsf_w, head_w, offs, out)
         nc.vector.memset(ones[:], 1.0)
         eps = held.tile([P, 1], F32, name="eps")
         nc.vector.memset(eps[:], EPS)
+        warmed = held.tile([P, 1], F32, name="warmed")
+        nc.scalar.activation(warmed[:], eps[:], ACT.Abs_reciprocal_sqrt)
 
         def embed(k):
             x = pieces.tile([P, CB, PIECE], F32, name="x")

@@ -21,11 +21,14 @@ def tile_metajanusrrpram_kernel(tc, tok_emb, pos_emb, rmsf_w, head_w, offs, out)
         tc.tile_pool(name="pieces", bufs=NP) as pieces,
         tc.psum_pool(name="psum", bufs=2) as psum,
     ):
+        tok_blocks = tok_emb.rearrange("(p b) s -> p b s", b=CB)
+        pos_blocks = pos_emb.rearrange("(p b) j -> p b j", b=CB)
+        head_blocks = head_w.rearrange("(p b) v -> p b v", b=CB)
+
         offsets = held.tile([P, N // 16], U16, name="offsets")
         nc.sync.dma_start(offsets[:], offs)
         gain = held.tile([P, CB], F32, name="gain")
-        with nc.allow_non_contiguous_dma(reason="768 gains, one to a partition and block"):
-            nc.sync.dma_start(gain[:], rmsf_w.rearrange("(b p) o -> p (b o)", p=P))
+        nc.sync.dma_start(gain[:], rmsf_w.rearrange("(p b) o -> p (b o)", b=CB))
 
         tables = [held.tile([P, S], F32, name=f"table{b}") for b in range(CB)]
         pos = [held.tile([P, CB, PIECE], F32, name=f"pos{k}") for k in range(NP)]
@@ -33,12 +36,10 @@ def tile_metajanusrrpram_kernel(tc, tok_emb, pos_emb, rmsf_w, head_w, offs, out)
         for k in range(NP):
             for b in range(CB):
                 if k == 0:
-                    nc.sync.dma_start(tables[b][:], tok_emb[b * P : (b + 1) * P, :])
-                nc.sync.dma_start(
-                    pos[k][:, b, :], pos_emb[b * P : (b + 1) * P, k * PIECE : (k + 1) * PIECE]
-                )
-            if k == 1:
-                nc.sync.dma_start(head[:], head_w.rearrange("(b p) v -> p b v", p=P))
+                    nc.sync.dma_start(tables[b][:], tok_blocks[:, b, :])
+                nc.sync.dma_start(pos[k][:, b, :], pos_blocks[:, b, k * PIECE : (k + 1) * PIECE])
+            if k == 0:
+                nc.sync.dma_start(head[:], head_blocks)
 
         ones = held.tile([P, P], BF16, name="ones")
         nc.vector.memset(ones[:], 1.0)

@@ -38,8 +38,8 @@ def tile_metajanusrrpram_kernel(tc, tok_emb, pos_emb, rmsf_w, head_w, offs, out)
                 if k == 0:
                     nc.sync.dma_start(tables[b][:], tok_blocks[:, b, :])
                 nc.sync.dma_start(pos[k][:, b, :], pos_blocks[:, b, k * PIECE : (k + 1) * PIECE])
-            if k == 0:
-                nc.sync.dma_start(head[:], head_blocks)
+                if k == 1:
+                    nc.sync.dma_start(head[:, b, :], head_blocks[:, b, :])
 
         ones = held.tile([P, P], BF16, name="ones")
         nc.vector.memset(ones[:], 1.0)

@@ -10,7 +10,8 @@ EPS = 1e-5
 CB = C // P
 VB = M // P
 PIECE = S
-NP = N // PIECE
+SPAN = 512
+NS = N // SPAN
 FLOPS = 2 * C * M * N
 
 
@@ -18,28 +19,28 @@ def tile_metajanusrrpram_kernel(tc, tok_emb, pos_emb, rmsf_w, head_w, offs, out)
     nc = tc.nc
     with (
         tc.tile_pool(name="held", bufs=1) as held,
-        tc.tile_pool(name="pieces", bufs=NP) as pieces,
-        tc.psum_pool(name="psum", bufs=2) as psum,
+        tc.tile_pool(name="spans", bufs=NS) as spans,
+        tc.psum_pool(name="psum", bufs=NS) as psum,
     ):
         tok_blocks = tok_emb.rearrange("(p b) s -> p b s", b=CB)
         pos_blocks = pos_emb.rearrange("(p b) j -> p b j", b=CB)
         head_blocks = head_w.rearrange("(p b) v -> p b v", b=CB)
+        gain_blocks = rmsf_w.rearrange("(p b) o -> p (b o)", b=CB)
 
         offsets = held.tile([P, N // 16], U16, name="offsets")
         nc.sync.dma_start(offsets[:], offs)
         gain = held.tile([P, CB], F32, name="gain")
-        nc.sync.dma_start(gain[:], rmsf_w.rearrange("(p b) o -> p (b o)", b=CB))
-
+        nc.sync.dma_start(gain[:], gain_blocks)
         tables = [held.tile([P, S], F32, name=f"table{b}") for b in range(CB)]
-        pos = [held.tile([P, CB, PIECE], F32, name=f"pos{k}") for k in range(NP)]
+        pos = [held.tile([P, CB, SPAN], F32, name=f"pos{i}") for i in range(NS)]
         head = held.tile([P, CB, M], BF16, name="head")
-        for k in range(NP):
+        for b in range(CB):
+            nc.sync.dma_start(tables[b][:], tok_blocks[:, b, :])
+            nc.sync.dma_start(pos[0][:, b, :], pos_blocks[:, b, 0:SPAN])
+        nc.sync.dma_start(head[:], head_blocks)
+        for i in range(1, NS):
             for b in range(CB):
-                if k == 0:
-                    nc.sync.dma_start(tables[b][:], tok_blocks[:, b, :])
-                nc.sync.dma_start(pos[k][:, b, :], pos_blocks[:, b, k * PIECE : (k + 1) * PIECE])
-                if k == 1:
-                    nc.sync.dma_start(head[:, b, :], head_blocks[:, b, :])
+                nc.sync.dma_start(pos[i][:, b, :], pos_blocks[:, b, i * SPAN : (i + 1) * SPAN])
 
         ones = held.tile([P, P], BF16, name="ones")
         nc.vector.memset(ones[:], 1.0)
@@ -48,18 +49,22 @@ def tile_metajanusrrpram_kernel(tc, tok_emb, pos_emb, rmsf_w, head_w, offs, out)
         warmed = held.tile([P, 1], F32, name="warmed")
         nc.scalar.activation(warmed[:], eps[:], ACT.Abs_reciprocal_sqrt)
 
-        def embed(k):
-            x = pieces.tile([P, CB, PIECE], F32, name="x")
-            squares = pieces.tile([P, CB, PIECE], BF16, name="squares")
-            gained = pieces.tile([P, CB, PIECE], BF16, name="gained")
-            sumsq = psum.tile([P, PIECE], F32, name="sumsq")
-            logits = [psum.tile([P, PIECE], F32, name=f"logits{v}") for v in range(VB)]
-            piece_offsets = offsets[:, k * (PIECE // 16) : (k + 1) * (PIECE // 16)]
+        def embed(i):
+            x = spans.tile([P, CB, SPAN], F32, name="x")
+            squares = spans.tile([P, CB, SPAN], BF16, name="squares")
+            gained = spans.tile([P, CB, SPAN], BF16, name="gained")
+            sumsq = psum.tile([P, SPAN], F32, name="sumsq")
+            logits = [psum.tile([P, SPAN], F32, name=f"logits{v}") for v in range(VB)]
             for b in range(CB):
                 first, last = b == 0, b == CB - 1
-                nc.vector.tensor_tensor(
-                    x[:, b, :], tables[b][:].indirect(piece_offsets), pos[k][:, b, :], ADD
-                )
+                for lo in range(0, SPAN, PIECE):
+                    column = (i * SPAN + lo) // 16
+                    nc.vector.tensor_tensor(
+                        x[:, b, lo : lo + PIECE],
+                        tables[b][:].indirect(offsets[:, column : column + PIECE // 16]),
+                        pos[i][:, b, lo : lo + PIECE],
+                        ADD,
+                    )
                 nc.scalar.activation(squares[:, b, :], x[:, b, :], ACT.Square)
                 nc.scalar.activation(gained[:, b, :], x[:, b, :], ACT.Copy, scale=gain[:, b : b + 1])
                 nc.tensor.matmul(sumsq[:], ones[:], squares[:, b, :], start=first, stop=last)
@@ -67,18 +72,16 @@ def tile_metajanusrrpram_kernel(tc, tok_emb, pos_emb, rmsf_w, head_w, offs, out)
                     nc.tensor.matmul(
                         logits[v][:], head[:, b, v * P : (v + 1) * P], gained[:, b, :], start=first, stop=last
                     )
-            r = pieces.tile([P, PIECE], F32, name="r")
+            r = spans.tile([P, SPAN], F32, name="r")
             nc.scalar.activation(r[:], sumsq[:], ACT.Abs_reciprocal_sqrt, bias=eps[:], scale=1.0 / C)
             return r, logits
 
-        def normalise(k, r, logits):
+        def normalise(i, r, logits):
             for v in range(VB):
-                staged = pieces.tile([P, PIECE], F32, name=f"staged{v}")
+                staged = spans.tile([P, SPAN], F32, name=f"staged{v}")
                 nc.vector.tensor_tensor(staged[:], logits[v][:], r[:], MULT)
-                nc.sync.dma_start(out[v * P : (v + 1) * P, k * PIECE : (k + 1) * PIECE], staged[:])
+                nc.sync.dma_start(out[v * P : (v + 1) * P, i * SPAN : (i + 1) * SPAN], staged[:])
 
-        embedded = embed(0)
-        for k in range(NP):
-            following = embed(k + 1) if k + 1 < NP else None
-            normalise(k, *embedded)
-            embedded = following
+        embedded = [embed(i) for i in range(NS)]
+        for i in range(NS):
+            normalise(i, *embedded[i])

@@ -55,6 +55,7 @@ def tile_metajanusrrpram_kernel(tc, tok_emb, pos_emb, rmsf_w, head_w, offs, out)
             gained = spans.tile([P, CB, SPAN], BF16, name="gained")
             sumsq = psum.tile([P, SPAN], F32, name="sumsq")
             logits = [psum.tile([P, SPAN], F32, name=f"logits{v}") for v in range(VB)]
+            step = PIECE if i == NS - 1 else SPAN
             for b in range(CB):
                 first, last = b == 0, b == CB - 1
                 for lo in range(0, SPAN, PIECE):
@@ -65,22 +66,35 @@ def tile_metajanusrrpram_kernel(tc, tok_emb, pos_emb, rmsf_w, head_w, offs, out)
                         pos[i][:, b, lo : lo + PIECE],
                         ADD,
                     )
-                nc.scalar.activation(squares[:, b, :], x[:, b, :], ACT.Square)
-                nc.scalar.activation(gained[:, b, :], x[:, b, :], ACT.Copy, scale=gain[:, b : b + 1])
+                for lo in range(0, SPAN, step):
+                    nc.scalar.activation(squares[:, b, lo : lo + step], x[:, b, lo : lo + step], ACT.Square)
+                for lo in range(0, SPAN, step):
+                    nc.scalar.activation(
+                        gained[:, b, lo : lo + step], x[:, b, lo : lo + step], ACT.Copy, scale=gain[:, b : b + 1]
+                    )
                 nc.tensor.matmul(sumsq[:], ones[:], squares[:, b, :], start=first, stop=last)
                 for v in range(VB):
                     nc.tensor.matmul(
                         logits[v][:], head[:, b, v * P : (v + 1) * P], gained[:, b, :], start=first, stop=last
                     )
             r = spans.tile([P, SPAN], F32, name="r")
-            nc.scalar.activation(r[:], sumsq[:], ACT.Abs_reciprocal_sqrt, bias=eps[:], scale=1.0 / C)
+            for lo in range(0, SPAN, step):
+                nc.scalar.activation(
+                    r[:, lo : lo + step], sumsq[:, lo : lo + step], ACT.Abs_reciprocal_sqrt, bias=eps[:], scale=1.0 / C
+                )
             return r, logits
 
         def normalise(i, r, logits):
-            for v in range(VB):
-                staged = spans.tile([P, SPAN], F32, name=f"staged{v}")
-                nc.vector.tensor_tensor(staged[:], logits[v][:], r[:], MULT)
-                nc.sync.dma_start(out[v * P : (v + 1) * P, i * SPAN : (i + 1) * SPAN], staged[:])
+            step = PIECE if i == NS - 1 else SPAN
+            staged = [spans.tile([P, SPAN], F32, name=f"staged{v}") for v in range(VB)]
+            for lo in range(0, SPAN, step):
+                for v in range(VB):
+                    nc.vector.tensor_tensor(
+                        staged[v][:, lo : lo + step], logits[v][:, lo : lo + step], r[:, lo : lo + step], MULT
+                    )
+                    nc.sync.dma_start(
+                        out[v * P : (v + 1) * P, i * SPAN + lo : i * SPAN + lo + step], staged[v][:, lo : lo + step]
+                    )
 
         embedded = [embed(i) for i in range(NS)]
         for i in range(NS):

@@ -10,17 +10,24 @@ EPS = 1e-5
 CB = C // P
 VB = M // P
 PIECE = S
-SPAN = 512
-NS = N // SPAN
+BANK = 512
+HALF = N // 2
+SPANS = ((0, 512), (512, 256), (768, 256))
+NS = len(SPANS)
+EARLY = 2
 FLOPS = 2 * C * M * N
 
 
 def tile_metajanusrrpram_kernel(tc, tok_emb, pos_emb, rmsf_w, head_w, offs, out):
     nc = tc.nc
+    units = (
+        [(b, i) for b in range(EARLY) for i in range(NS)]
+        + [(b, 0) for b in range(EARLY, CB)]
+        + [(b, i) for b in range(EARLY, CB) for i in range(1, NS)]
+    )
     with (
         tc.tile_pool(name="held", bufs=1) as held,
-        tc.tile_pool(name="spans", bufs=NS) as spans,
-        tc.psum_pool(name="psum", bufs=NS) as psum,
+        tc.psum_pool(name="psum", bufs=1) as psum,
     ):
         tok_blocks = tok_emb.rearrange("(p b) s -> p b s", b=CB)
         pos_blocks = pos_emb.rearrange("(p b) j -> p b j", b=CB)
@@ -32,15 +39,17 @@ def tile_metajanusrrpram_kernel(tc, tok_emb, pos_emb, rmsf_w, head_w, offs, out)
         gain = held.tile([P, CB], F32, name="gain")
         nc.sync.dma_start(gain[:], gain_blocks)
         tables = [held.tile([P, S], F32, name=f"table{b}") for b in range(CB)]
-        pos = [held.tile([P, CB, SPAN], F32, name=f"pos{i}") for i in range(NS)]
+        pos = [[held.tile([P, HALF], F32, name=f"pos{b}_{h}") for h in range(2)] for b in range(CB)]
         head = held.tile([P, CB, M], BF16, name="head")
-        for b in range(CB):
-            nc.sync.dma_start(tables[b][:], tok_blocks[:, b, :])
-            nc.sync.dma_start(pos[0][:, b, :], pos_blocks[:, b, 0:SPAN])
-        nc.sync.dma_start(head[:], head_blocks)
-        for i in range(1, NS):
-            for b in range(CB):
-                nc.sync.dma_start(pos[i][:, b, :], pos_blocks[:, b, i * SPAN : (i + 1) * SPAN])
+        for b, i in units:
+            if i == 0:
+                nc.sync.dma_start(tables[b][:], tok_blocks[:, b, :])
+            if i < 2:
+                width = PIECE if (b, i) == units[0] else HALF
+                for lo in range(0, HALF, width):
+                    nc.sync.dma_start(pos[b][i][:, lo : lo + width], pos_blocks[:, b, i * HALF + lo : i * HALF + lo + width])
+            if (b, i) == (1, 1):
+                nc.sync.dma_start(head[:], head_blocks)
 
         ones = held.tile([P, P], BF16, name="ones")
         nc.vector.memset(ones[:], 1.0)
@@ -49,53 +58,58 @@ def tile_metajanusrrpram_kernel(tc, tok_emb, pos_emb, rmsf_w, head_w, offs, out)
         warmed = held.tile([P, 1], F32, name="warmed")
         nc.scalar.activation(warmed[:], eps[:], ACT.Abs_reciprocal_sqrt)
 
-        def embed(i):
-            x = spans.tile([P, CB, SPAN], F32, name="x")
-            squares = spans.tile([P, CB, SPAN], BF16, name="squares")
-            gained = spans.tile([P, CB, SPAN], BF16, name="gained")
-            sumsq = psum.tile([P, SPAN], F32, name="sumsq")
-            logits = [psum.tile([P, SPAN], F32, name=f"logits{v}") for v in range(VB)]
-            step = PIECE if i == NS - 1 else SPAN
-            for b in range(CB):
-                first, last = b == 0, b == CB - 1
-                for lo in range(0, SPAN, PIECE):
-                    column = (i * SPAN + lo) // 16
-                    nc.vector.tensor_tensor(
-                        x[:, b, lo : lo + PIECE],
-                        tables[b][:].indirect(offsets[:, column : column + PIECE // 16]),
-                        pos[i][:, b, lo : lo + PIECE],
-                        ADD,
-                    )
-                for lo in range(0, SPAN, step):
-                    nc.scalar.activation(squares[:, b, lo : lo + step], x[:, b, lo : lo + step], ACT.Square)
-                for lo in range(0, SPAN, step):
-                    nc.scalar.activation(
-                        gained[:, b, lo : lo + step], x[:, b, lo : lo + step], ACT.Copy, scale=gain[:, b : b + 1]
-                    )
-                nc.tensor.matmul(sumsq[:], ones[:], squares[:, b, :], start=first, stop=last)
-                for v in range(VB):
-                    nc.tensor.matmul(
-                        logits[v][:], head[:, b, v * P : (v + 1) * P], gained[:, b, :], start=first, stop=last
-                    )
-            r = spans.tile([P, SPAN], F32, name="r")
-            for lo in range(0, SPAN, step):
-                nc.scalar.activation(
-                    r[:, lo : lo + step], sumsq[:, lo : lo + step], ACT.Abs_reciprocal_sqrt, bias=eps[:], scale=1.0 / C
+        x = held.tile([P, CB, N], F32, name="x")
+        squares = held.tile([P, CB, N], BF16, name="squares")
+        gained = held.tile([P, CB, N], BF16, name="gained")
+        r = held.tile([P, N], F32, name="r")
+        logits = [[psum.tile([P, BANK], F32, name=f"logits{i}_{v}") for v in range(VB)] for i in range(NS)]
+        sumsq = [psum.tile([P, BANK], F32, name=f"sumsq{i}") for i in range(NS - 1)]
+
+        def tokens_of(i):
+            return slice(SPANS[i][0], SPANS[i][0] + SPANS[i][1])
+
+        def add_squares(b, i):
+            nc.tensor.matmul(
+                sumsq[i][:, 0 : SPANS[i][1]], ones[:], squares[:, b, tokens_of(i)], start=b == 0, stop=b == CB - 1
+            )
+
+        def root(i):
+            nc.scalar.activation(
+                r[:, tokens_of(i)], sumsq[i][:, 0 : SPANS[i][1]], ACT.Abs_reciprocal_sqrt, bias=eps[:], scale=1.0 / C
+            )
+
+        for b, i in units:
+            tokens = tokens_of(i)
+            for lo in range(tokens.start, tokens.stop, PIECE):
+                nc.vector.tensor_tensor(
+                    x[:, b, lo : lo + PIECE],
+                    tables[b][:].indirect(offsets[:, lo // 16 : (lo + PIECE) // 16]),
+                    pos[b][lo // HALF][:, lo % HALF : lo % HALF + PIECE],
+                    ADD,
                 )
-            return r, logits
+            nc.scalar.activation(squares[:, b, tokens], x[:, b, tokens], ACT.Square)
+            nc.scalar.activation(gained[:, b, tokens], x[:, b, tokens], ACT.Copy, scale=gain[:, b : b + 1])
+            if (b, i) == (EARLY, 1):
+                root(0)
+                sumsq.append(psum.tile([P, BANK], F32, name=f"sumsq{NS - 1}", tag="sumsq0"))
+                for early in range(EARLY):
+                    add_squares(early, NS - 1)
+            if i < NS - 1 or b >= EARLY:
+                add_squares(b, i)
+            for v in range(VB):
+                nc.tensor.matmul(
+                    logits[i][v][:, 0 : SPANS[i][1]],
+                    head[:, b, v * P : (v + 1) * P],
+                    gained[:, b, tokens],
+                    start=b == 0,
+                    stop=b == CB - 1,
+                )
+            if b == CB - 1 and i > 0:
+                root(i)
 
-        def normalise(i, r, logits):
-            step = PIECE if i == NS - 1 else SPAN
-            staged = [spans.tile([P, SPAN], F32, name=f"staged{v}") for v in range(VB)]
-            for lo in range(0, SPAN, step):
-                for v in range(VB):
-                    nc.vector.tensor_tensor(
-                        staged[v][:, lo : lo + step], logits[v][:, lo : lo + step], r[:, lo : lo + step], MULT
-                    )
-                    nc.sync.dma_start(
-                        out[v * P : (v + 1) * P, i * SPAN + lo : i * SPAN + lo + step], staged[v][:, lo : lo + step]
-                    )
-
-        embedded = [embed(i) for i in range(NS)]
+        staged = held.tile([P, VB, N], F32, name="staged", tag=f"pos{CB - 1}_1")
         for i in range(NS):
-            normalise(i, *embedded[i])
+            tokens = tokens_of(i)
+            for v in range(VB):
+                nc.vector.tensor_tensor(staged[:, v, tokens], logits[i][v][:, 0 : SPANS[i][1]], r[:, tokens], MULT)
+                nc.sync.dma_start(out[v * P : (v + 1) * P, tokens], staged[:, v, tokens])

@@ -81,14 +81,15 @@ def tile_metajanusrrpram_kernel(tc, tok_emb, pos_emb, rmsf_w, head_w, offs, out)
         for b, i in units:
             tokens = tokens_of(i)
             for lo in range(tokens.start, tokens.stop, PIECE):
+                piece = slice(lo, lo + PIECE)
                 nc.vector.tensor_tensor(
-                    x[:, b, lo : lo + PIECE],
+                    x[:, b, piece],
                     tables[b][:].indirect(offsets[:, lo // 16 : (lo + PIECE) // 16]),
                     pos[b][lo // HALF][:, lo % HALF : lo % HALF + PIECE],
                     ADD,
                 )
-            nc.scalar.activation(squares[:, b, tokens], x[:, b, tokens], ACT.Square)
-            nc.scalar.activation(gained[:, b, tokens], x[:, b, tokens], ACT.Copy, scale=gain[:, b : b + 1])
+                nc.scalar.activation(squares[:, b, piece], x[:, b, piece], ACT.Square)
+                nc.scalar.activation(gained[:, b, piece], x[:, b, piece], ACT.Copy, scale=gain[:, b : b + 1])
             if (b, i) == (EARLY, 1):
                 root(0)
                 sumsq.append(psum.tile([P, BANK], F32, name=f"sumsq{NS - 1}", tag="sumsq0"))

@@ -37,7 +37,6 @@ def tile_metajanusrrpram_kernel(tc, tok_emb, pos_emb, rmsf_w, head_w, offs, out)
         offsets = held.tile([P, N // 16], U16, name="offsets")
         nc.sync.dma_start(offsets[:], offs)
         gain = held.tile([P, CB], F32, name="gain")
-        nc.sync.dma_start(gain[:], gain_blocks)
         tables = [held.tile([P, S], F32, name=f"table{b}") for b in range(CB)]
         pos = [[held.tile([P, HALF], F32, name=f"pos{b}_{h}") for h in range(2)] for b in range(CB)]
         head = held.tile([P, CB, M], BF16, name="head")
@@ -48,8 +47,12 @@ def tile_metajanusrrpram_kernel(tc, tok_emb, pos_emb, rmsf_w, head_w, offs, out)
                 width = PIECE if (b, i) == units[0] else HALF
                 for lo in range(0, HALF, width):
                     nc.sync.dma_start(pos[b][i][:, lo : lo + width], pos_blocks[:, b, i * HALF + lo : i * HALF + lo + width])
-            if (b, i) == (1, 1):
-                nc.sync.dma_start(head[:], head_blocks)
+            if (b, i) == units[0]:
+                nc.sync.dma_start(gain[:], gain_blocks)
+            if (b, i) == (EARLY - 1, 1):
+                nc.sync.dma_start(head[:, 0 : CB // 2, :], head_blocks[:, 0 : CB // 2, :])
+            if (b, i) == (CB // 2 + 1, 0):
+                nc.sync.dma_start(head[:, CB // 2 : CB, :], head_blocks[:, CB // 2 : CB, :])
 
         ones = held.tile([P, P], BF16, name="ones")
         nc.vector.memset(ones[:], 1.0)

@@ -65,6 +65,7 @@ def tile_metajanusrrpram_kernel(tc, tok_emb, pos_emb, rmsf_w, head_w, offs, out)
         squares = held.tile([P, CB, N], BF16, name="squares")
         gained = held.tile([P, CB, N], BF16, name="gained")
         r = held.tile([P, N], F32, name="r")
+        shared = held.tile([P, PIECE], F32, name="shared")
         logits = [[psum.tile([P, BANK], F32, name=f"logits{i}_{v}") for v in range(VB)] for i in range(NS)]
         sumsq = [psum.tile([P, BANK], F32, name=f"sumsq{i}") for i in range(NS - 1)]
 
@@ -95,6 +96,7 @@ def tile_metajanusrrpram_kernel(tc, tok_emb, pos_emb, rmsf_w, head_w, offs, out)
                 nc.scalar.activation(gained[:, b, piece], x[:, b, piece], ACT.Copy, scale=gain[:, b : b + 1])
             if (b, i) == (EARLY, 1):
                 root(0)
+                nc.scalar.copy(shared[:], logits[0][VB - 1][:, BANK - PIECE : BANK])
                 sumsq.append(psum.tile([P, BANK], F32, name=f"sumsq{NS - 1}", tag="sumsq0"))
                 for early in range(EARLY):
                     add_squares(early, NS - 1)
@@ -112,8 +114,12 @@ def tile_metajanusrrpram_kernel(tc, tok_emb, pos_emb, rmsf_w, head_w, offs, out)
                 root(i)
 
         staged = held.tile([P, VB, N], F32, name="staged", tag=f"pos{CB - 1}_1")
+        share = slice(BANK - PIECE, BANK)
+        nc.gpsimd.tensor_tensor(staged[:, VB - 1, share], shared[:], r[:, share], MULT)
+        nc.sync.dma_start(out[(VB - 1) * P : VB * P, share], staged[:, VB - 1, share])
         for i in range(NS):
-            tokens = tokens_of(i)
             for v in range(VB):
-                nc.vector.tensor_tensor(staged[:, v, tokens], logits[i][v][:, 0 : SPANS[i][1]], r[:, tokens], MULT)
+                width = SPANS[i][1] - PIECE if (i, v) == (0, VB - 1) else SPANS[i][1]
+                tokens = slice(SPANS[i][0], SPANS[i][0] + width)
+                nc.vector.tensor_tensor(staged[:, v, tokens], logits[i][v][:, 0:width], r[:, tokens], MULT)
                 nc.sync.dma_start(out[v * P : (v + 1) * P, tokens], staged[:, v, tokens])

@@ -65,7 +65,6 @@ def tile_metajanusrrpram_kernel(tc, tok_emb, pos_emb, rmsf_w, head_w, offs, out)
         squares = held.tile([P, CB, N], BF16, name="squares")
         gained = held.tile([P, CB, N], BF16, name="gained")
         r = held.tile([P, N], F32, name="r")
-        shared = held.tile([P, PIECE], F32, name="shared")
         logits = [[psum.tile([P, BANK], F32, name=f"logits{i}_{v}") for v in range(VB)] for i in range(NS)]
         sumsq = [psum.tile([P, BANK], F32, name=f"sumsq{i}") for i in range(NS - 1)]
 
@@ -96,7 +95,6 @@ def tile_metajanusrrpram_kernel(tc, tok_emb, pos_emb, rmsf_w, head_w, offs, out)
                 nc.scalar.activation(gained[:, b, piece], x[:, b, piece], ACT.Copy, scale=gain[:, b : b + 1])
             if (b, i) == (EARLY, 1):
                 root(0)
-                nc.scalar.copy(shared[:], logits[0][VB - 1][:, BANK - PIECE : BANK])
                 sumsq.append(psum.tile([P, BANK], F32, name=f"sumsq{NS - 1}", tag="sumsq0"))
                 for early in range(EARLY):
                     add_squares(early, NS - 1)
@@ -113,13 +111,11 @@ def tile_metajanusrrpram_kernel(tc, tok_emb, pos_emb, rmsf_w, head_w, offs, out)
             if b == CB - 1 and i > 0:
                 root(i)
 
-        staged = held.tile([P, VB, N], F32, name="staged", tag=f"pos{CB - 1}_1")
-        share = slice(BANK - PIECE, BANK)
-        nc.gpsimd.tensor_tensor(staged[:, VB - 1, share], shared[:], r[:, share], MULT)
-        nc.sync.dma_start(out[(VB - 1) * P : VB * P, share], staged[:, VB - 1, share])
+        staged = held.tile([P, VB, N - HALF], F32, name="staged")
         for i in range(NS):
             for v in range(VB):
-                width = SPANS[i][1] - PIECE if (i, v) == (0, VB - 1) else SPANS[i][1]
-                tokens = slice(SPANS[i][0], SPANS[i][0] + width)
-                nc.vector.tensor_tensor(staged[:, v, tokens], logits[i][v][:, 0:width], r[:, tokens], MULT)
-                nc.sync.dma_start(out[v * P : (v + 1) * P, tokens], staged[:, v, tokens])
+                first, width = SPANS[i]
+                tokens = slice(first, first + width)
+                result = pos[CB - 1 - v][1][:] if i == 0 else staged[:, v, first - HALF : first - HALF + width]
+                nc.vector.tensor_tensor(result, logits[i][v][:, 0:width], r[:, tokens], MULT)
+                nc.sync.dma_start(out[v * P : (v + 1) * P, tokens], result)

import concourse.mybir as mybir

F32, BF16, U16 = mybir.dt.float32, mybir.dt.bfloat16, mybir.dt.uint16
ADD, MULT = mybir.AluOpType.add, mybir.AluOpType.mult
ACT = mybir.ActivationFunctionType

P = 128
C, S, N, M = 768, 256, 1024, 256
EPS = 1e-5
CB = C // P
VB = M // P
PIECE = S
BANK = 512
HALF = N // 2
SPANS = ((0, 512), (512, 256), (768, 256))
NS = len(SPANS)
EARLY = 2
FLOPS = 2 * C * M * N


def tile_metajanusrrpram_kernel(tc, tok_emb, pos_emb, rmsf_w, head_w, offs, out):
    nc = tc.nc
    units = (
        [(b, i) for b in range(EARLY) for i in range(NS)]
        + [(b, 0) for b in range(EARLY, CB)]
        + [(b, i) for b in range(EARLY, CB) for i in range(1, NS)]
    )
    with (
        tc.tile_pool(name="held", bufs=1) as held,
        tc.psum_pool(name="psum", bufs=1) as psum,
    ):
        tok_blocks = tok_emb.rearrange("(p b) s -> p b s", b=CB)
        pos_blocks = pos_emb.rearrange("(p b) j -> p b j", b=CB)
        head_blocks = head_w.rearrange("(p b) v -> p b v", b=CB)
        gain_blocks = rmsf_w.rearrange("(p b) o -> p (b o)", b=CB)

        offsets = held.tile([P, N // 16], U16, name="offsets")
        nc.sync.dma_start(offsets[:], offs)
        gain = held.tile([P, CB], F32, name="gain")
        tables = [held.tile([P, S], F32, name=f"table{b}") for b in range(CB)]
        pos = [[held.tile([P, HALF], F32, name=f"pos{b}_{h}") for h in range(2)] for b in range(CB)]
        head = held.tile([P, CB, M], BF16, name="head")
        for b, i in units:
            if i == 0:
                nc.sync.dma_start(tables[b][:], tok_blocks[:, b, :])
            if i < 2:
                width = PIECE if (b, i) == units[0] else HALF
                for lo in range(0, HALF, width):
                    nc.sync.dma_start(pos[b][i][:, lo : lo + width], pos_blocks[:, b, i * HALF + lo : i * HALF + lo + width])
            if (b, i) == units[0]:
                nc.sync.dma_start(gain[:], gain_blocks)
            if (b, i) == (EARLY - 1, 1):
                nc.sync.dma_start(head[:, 0 : CB // 2, :], head_blocks[:, 0 : CB // 2, :])
            if (b, i) == (CB // 2 + 1, 0):
                nc.sync.dma_start(head[:, CB // 2 : CB, :], head_blocks[:, CB // 2 : CB, :])

        ones = held.tile([P, P], BF16, name="ones")
        nc.vector.memset(ones[:], 1.0)
        eps = held.tile([P, 1], F32, name="eps")
        nc.vector.memset(eps[:], EPS)
        warmed = held.tile([P, 1], F32, name="warmed")
        nc.scalar.activation(warmed[:], eps[:], ACT.Abs_reciprocal_sqrt)

        x = held.tile([P, CB, N], F32, name="x")
        squares = held.tile([P, CB, N], BF16, name="squares")
        gained = held.tile([P, CB, N], BF16, name="gained")
        r = held.tile([P, N], F32, name="r")
        logits = [[psum.tile([P, BANK], F32, name=f"logits{i}_{v}") for v in range(VB)] for i in range(NS)]
        sumsq = [psum.tile([P, BANK], F32, name=f"sumsq{i}") for i in range(NS - 1)]

        def tokens_of(i):
            return slice(SPANS[i][0], SPANS[i][0] + SPANS[i][1])

        def add_squares(b, i):
            nc.tensor.matmul(
                sumsq[i][:, 0 : SPANS[i][1]], ones[:], squares[:, b, tokens_of(i)], start=b == 0, stop=b == CB - 1
            )

        def root(i):
            nc.scalar.activation(
                r[:, tokens_of(i)], sumsq[i][:, 0 : SPANS[i][1]], ACT.Abs_reciprocal_sqrt, bias=eps[:], scale=1.0 / C
            )

        for b, i in units:
            tokens = tokens_of(i)
            for lo in range(tokens.start, tokens.stop, PIECE):
                piece = slice(lo, lo + PIECE)
                nc.vector.tensor_tensor(
                    x[:, b, piece],
                    tables[b][:].indirect(offsets[:, lo // 16 : (lo + PIECE) // 16]),
                    pos[b][lo // HALF][:, lo % HALF : lo % HALF + PIECE],
                    ADD,
                )
                nc.scalar.activation(squares[:, b, piece], x[:, b, piece], ACT.Square)
                nc.scalar.activation(gained[:, b, piece], x[:, b, piece], ACT.Copy, scale=gain[:, b : b + 1])
            if (b, i) == (EARLY, 1):
                root(0)
                sumsq.append(psum.tile([P, BANK], F32, name=f"sumsq{NS - 1}", tag="sumsq0"))
                for early in range(EARLY):
                    add_squares(early, NS - 1)
            if i < NS - 1 or b >= EARLY:
                add_squares(b, i)
            for v in range(VB):
                nc.tensor.matmul(
                    logits[i][v][:, 0 : SPANS[i][1]],
                    head[:, b, v * P : (v + 1) * P],
                    gained[:, b, tokens],
                    start=b == 0,
                    stop=b == CB - 1,
                )
            if b == CB - 1 and i > 0:
                root(i)

        staged = held.tile([P, VB, N - HALF], F32, name="staged")
        for i in range(NS):
            for v in range(VB):
                first, width = SPANS[i]
                tokens = slice(first, first + width)
                result = pos[CB - 1 - v][1][:] if i == 0 else staged[:, v, first - HALF : first - HALF + width]
                nc.vector.tensor_tensor(result, logits[i][v][:, 0:width], r[:, tokens], MULT)
                nc.sync.dma_start(out[v * P : (v + 1) * P, tokens], result)
